import numpy as np
import ml_dtypes

BF16 = ml_dtypes.bfloat16


def bf(x):
    return np.asarray(x, np.float32).astype(BF16)


def f32(x):
    return np.asarray(x, np.float32)


def f64(x):
    return np.asarray(x).astype(np.float64)


def striped(idx):
    return np.tile(idx.reshape(-1, 16).T, (8, 1))


D, S, M, N = 128, 512, 512, 128


def setup_inputs():
    return {"table": bf(0.1 * np.random.standard_normal((D, S))), "feat": bf(np.abs(np.random.standard_normal((D, M)))), "offs": striped(np.random.permutation(S)[:N])}


def reference(table, feat, offs):
    idx = offs[:16].T.reshape(-1)
    z = f64(feat).T @ f64(table)[:, idx]
    return 1.0 / (1.0 + np.exp(-z))

@@ -1,0 +1,39 @@
+import concourse.mybir as mybir
+
+BF16, F32, U16 = mybir.dt.bfloat16, mybir.dt.float32, mybir.dt.uint16
+SIGMOID = mybir.ActivationFunctionType.Sigmoid
+
+P = 128
+PLACES = 512
+OBJECTS = 128
+BLOCKS = PLACES // P
+
+FLOPS = 2 * P * PLACES * OBJECTS
+
+
+def tile_diceloss_kernel(tc, table, feat, offs, out):
+    nc = tc.nc
+    with (
+        tc.tile_pool(name="held", bufs=1) as held,
+        tc.tile_pool(name="results", bufs=BLOCKS) as results,
+        tc.psum_pool(name="psum", bufs=BLOCKS) as psum,
+    ):
+        HALF = PLACES // 2
+        filters = held.tile([P, PLACES], BF16, name="filters")
+        nc.sync.dma_start(filters[:], table)
+        halves = [held.tile([P, HALF], BF16, name=f"features{h}") for h in range(2)]
+        nc.sync.dma_start(halves[0][:], feat[:, 0:HALF])
+        offsets = held.tile([P, OBJECTS // 16], U16, name="offsets")
+        nc.sync.dma_start(offsets[:], offs)
+        nc.sync.dma_start(halves[1][:], feat[:, HALF:PLACES])
+        features = [half[:, c : c + P] for half in halves for c in (0, P)]
+
+        for b in range(BLOCKS):
+            places = slice(b * P, (b + 1) * P)
+            logits = psum.tile([P, OBJECTS], F32, name="logits")
+            nc.tensor.matmul(
+                logits[:], features[b], filters[:].indirect(offsets[:]), start=True, stop=True
+            )
+            values = results.tile([P, OBJECTS], F32, name="values")
+            nc.scalar.activation(values[:], logits[:], SIGMOID)
+            nc.sync.dma_start(out[places, :], values[:])

@@ -8,6 +8,8 @@ PLACES = 512
 OBJECTS = 128
 BLOCKS = PLACES // P
 
+ROW_ALIGN = 256
+
 FLOPS = 2 * P * PLACES * OBJECTS
 
 
@@ -19,11 +21,13 @@ def tile_diceloss_kernel(tc, table, feat, offs, out):
         tc.psum_pool(name="psum", bufs=BLOCKS) as psum,
     ):
         HALF = PLACES // 2
-        filters = held.tile([P, PLACES], BF16, name="filters")
+        filters = held.tile([P, PLACES], BF16, name="filters", align_bytes=ROW_ALIGN)
         nc.sync.dma_start(filters[:], table)
-        halves = [held.tile([P, HALF], BF16, name=f"features{h}") for h in range(2)]
+        halves = [
+            held.tile([P, HALF], BF16, name=f"features{h}", align_bytes=ROW_ALIGN) for h in range(2)
+        ]
         nc.sync.dma_start(halves[0][:], feat[:, 0:HALF])
-        offsets = held.tile([P, OBJECTS // 16], U16, name="offsets")
+        offsets = held.tile([P, OBJECTS // 16], U16, name="offsets", align_bytes=ROW_ALIGN)
         nc.sync.dma_start(offsets[:], offs)
         nc.sync.dma_start(halves[1][:], feat[:, HALF:PLACES])
         features = [half[:, c : c + P] for half in halves for c in (0, P)]
@@ -34,6 +38,6 @@ def tile_diceloss_kernel(tc, table, feat, offs, out):
             nc.tensor.matmul(
                 logits[:], features[b], filters[:].indirect(offsets[:]), start=True, stop=True
             )
-            values = results.tile([P, OBJECTS], F32, name="values")
+            values = results.tile([P, OBJECTS], F32, name="values", align_bytes=ROW_ALIGN)
             nc.scalar.activation(values[:], logits[:], SIGMOID)
             nc.sync.dma_start(out[places, :], values[:])

@@ -20,17 +20,15 @@ def tile_diceloss_kernel(tc, table, feat, offs, out):
         tc.tile_pool(name="results", bufs=BLOCKS) as results,
         tc.psum_pool(name="psum", bufs=BLOCKS) as psum,
     ):
-        HALF = PLACES // 2
         filters = held.tile([P, PLACES], BF16, name="filters", align_bytes=ROW_ALIGN)
         nc.sync.dma_start(filters[:], table)
-        halves = [
-            held.tile([P, HALF], BF16, name=f"features{h}", align_bytes=ROW_ALIGN) for h in range(2)
-        ]
-        nc.sync.dma_start(halves[0][:], feat[:, 0:HALF])
+        first = held.tile([P, P], BF16, name="first", align_bytes=ROW_ALIGN)
+        nc.sync.dma_start(first[:], feat[:, 0:P])
         offsets = held.tile([P, OBJECTS // 16], U16, name="offsets", align_bytes=ROW_ALIGN)
         nc.sync.dma_start(offsets[:], offs)
-        nc.sync.dma_start(halves[1][:], feat[:, HALF:PLACES])
-        features = [half[:, c : c + P] for half in halves for c in (0, P)]
+        rest = held.tile([P, PLACES - P], BF16, name="rest", align_bytes=ROW_ALIGN)
+        nc.sync.dma_start(rest[:], feat[:, P:PLACES])
+        features = [first[:]] + [rest[:, c : c + P] for c in range(0, PLACES - P, P)]
 
         for b in range(BLOCKS):
             places = slice(b * P, (b + 1) * P)

@@ -17,7 +17,7 @@ def tile_diceloss_kernel(tc, table, feat, offs, out):
     nc = tc.nc
     with (
         tc.tile_pool(name="held", bufs=1) as held,
-        tc.tile_pool(name="results", bufs=BLOCKS) as results,
+        tc.tile_pool(name="results", bufs=1) as results,
         tc.psum_pool(name="psum", bufs=BLOCKS) as psum,
     ):
         filters = held.tile([P, PLACES], BF16, name="filters", align_bytes=ROW_ALIGN)
@@ -26,16 +26,21 @@ def tile_diceloss_kernel(tc, table, feat, offs, out):
         nc.sync.dma_start(first[:], feat[:, 0:P])
         offsets = held.tile([P, OBJECTS // 16], U16, name="offsets", align_bytes=ROW_ALIGN)
         nc.sync.dma_start(offsets[:], offs)
-        rest = held.tile([P, PLACES - P], BF16, name="rest", align_bytes=ROW_ALIGN)
-        nc.sync.dma_start(rest[:], feat[:, P:PLACES])
-        features = [first[:]] + [rest[:, c : c + P] for c in range(0, PLACES - P, P)]
+        second = held.tile([P, P], BF16, name="second", align_bytes=ROW_ALIGN)
+        nc.sync.dma_start(second[:], feat[:, P : 2 * P])
+        rest = held.tile([P, 2 * P], BF16, name="rest", align_bytes=ROW_ALIGN)
+        nc.sync.dma_start(rest[:], feat[:, 2 * P : PLACES])
+        features = [first[:], second[:], rest[:, 0:P], rest[:, P : 2 * P]]
 
-        for b in range(BLOCKS):
-            places = slice(b * P, (b + 1) * P)
-            logits = psum.tile([P, OBJECTS], F32, name="logits")
-            nc.tensor.matmul(
-                logits[:], features[b], filters[:].indirect(offsets[:]), start=True, stop=True
-            )
-            values = results.tile([P, OBJECTS], F32, name="values", align_bytes=ROW_ALIGN)
-            nc.scalar.activation(values[:], logits[:], SIGMOID)
-            nc.sync.dma_start(out[places, :], values[:])
+        stores = [(0, 2), (2, 1), (3, 1)]
+
+        for first_block, blocks in stores:
+            values = results.tile([P, blocks, OBJECTS], F32, name=f"values{first_block}", align_bytes=ROW_ALIGN)
+            for k in range(blocks):
+                logits = psum.tile([P, OBJECTS], F32, name="logits")
+                nc.tensor.matmul(
+                    logits[:], features[first_block + k], filters[:].indirect(offsets[:]), start=True, stop=True
+                )
+                nc.scalar.activation(values[:, k, :], logits[:], SIGMOID)
+            places = slice(first_block * P, (first_block + blocks) * P)
+            nc.sync.dma_start(out[places, :].rearrange("(k p) j -> p k j", p=P), values[:])

@@ -8,7 +8,7 @@ PLACES = 512
 OBJECTS = 128
 BLOCKS = PLACES // P
 
-ROW_ALIGN = 256
+ROW_ALIGN = 1024
 
 FLOPS = 2 * P * PLACES * OBJECTS
 

import concourse.mybir as mybir

BF16, F32, U16 = mybir.dt.bfloat16, mybir.dt.float32, mybir.dt.uint16
SIGMOID = mybir.ActivationFunctionType.Sigmoid

P = 128
PLACES = 512
OBJECTS = 128
BLOCKS = PLACES // P

ROW_ALIGN = 1024

FLOPS = 2 * P * PLACES * OBJECTS


def tile_diceloss_kernel(tc, table, feat, offs, out):
    nc = tc.nc
    with (
        tc.tile_pool(name="held", bufs=1) as held,
        tc.tile_pool(name="results", bufs=1) as results,
        tc.psum_pool(name="psum", bufs=BLOCKS) as psum,
    ):
        filters = held.tile([P, PLACES], BF16, name="filters", align_bytes=ROW_ALIGN)
        nc.sync.dma_start(filters[:], table)
        first = held.tile([P, P], BF16, name="first", align_bytes=ROW_ALIGN)
        nc.sync.dma_start(first[:], feat[:, 0:P])
        offsets = held.tile([P, OBJECTS // 16], U16, name="offsets", align_bytes=ROW_ALIGN)
        nc.sync.dma_start(offsets[:], offs)
        second = held.tile([P, P], BF16, name="second", align_bytes=ROW_ALIGN)
        nc.sync.dma_start(second[:], feat[:, P : 2 * P])
        rest = held.tile([P, 2 * P], BF16, name="rest", align_bytes=ROW_ALIGN)
        nc.sync.dma_start(rest[:], feat[:, 2 * P : PLACES])
        features = [first[:], second[:], rest[:, 0:P], rest[:, P : 2 * P]]

        stores = [(0, 2), (2, 1), (3, 1)]

        for first_block, blocks in stores:
            values = results.tile([P, blocks, OBJECTS], F32, name=f"values{first_block}", align_bytes=ROW_ALIGN)
            for k in range(blocks):
                logits = psum.tile([P, OBJECTS], F32, name="logits")
                nc.tensor.matmul(
                    logits[:], features[first_block + k], filters[:].indirect(offsets[:]), start=True, stop=True
                )
                nc.scalar.activation(values[:, k, :], logits[:], SIGMOID)
            places = slice(first_block * P, (first_block + blocks) * P)
            nc.sync.dma_start(out[places, :].rearrange("(k p) j -> p k j", p=P), values[:])
